import numpy as np
import ml_dtypes

BF16 = ml_dtypes.bfloat16


def bf(x):
    return np.asarray(x, np.float32).astype(BF16)


def f32(x):
    return np.asarray(x, np.float32)


def f64(x):
    return np.asarray(x).astype(np.float64)


def striped(idx):
    return np.tile(idx.reshape(-1, 16).T, (8, 1))


V, D, M, N = 2048, 128, 256, 1024


def setup_inputs():
    return {"table": bf(np.random.standard_normal((D, V))), "w": bf(np.random.standard_normal((D, M - D)) / np.sqrt(D)), "offs": striped(np.random.permutation(np.tile(np.arange(V), 2))[:N])}


def reference(table, w, offs):
    idx = offs[:16].T.reshape(-1)
    x = f64(table)[:, idx]
    return np.concatenate([f64(w).T @ x, x], axis=0)

@@ -1,0 +1,45 @@
+import concourse.mybir as mybir
+from concourse.masks import make_identity
+
+BF16, F32, U16 = mybir.dt.bfloat16, mybir.dt.float32, mybir.dt.uint16
+COPY = mybir.ActivationFunctionType.Copy
+
+D = 128
+V = 2048
+N = 1024
+PIECE = 512
+PER_COLUMN = 16
+
+FLOPS = 2 * D * D * N
+
+
+def tile_documentgraph_kernel(tc, table, w, offs, out):
+    nc = tc.nc
+    with (
+        tc.tile_pool(name="held", bufs=1) as held,
+        tc.tile_pool(name="staging", bufs=4) as staging,
+        tc.psum_pool(name="banks", bufs=4) as banks,
+    ):
+        offsets = held.tile([D, N // PER_COLUMN], U16, name="offsets")
+        nc.sync.dma_start(offsets[:], offs)
+        window = held.tile([D, V], BF16, name="window")
+        nc.scalar.dma_start(window[:], table)
+        weights = held.tile([D, D], BF16, name="weights")
+        nc.sync.dma_start(weights[:], w)
+        identity = held.tile([D, D], BF16, name="identity")
+        make_identity(nc, identity[:])
+
+        for piece in range(N // PIECE):
+            columns = slice(piece * PIECE, (piece + 1) * PIECE)
+            piece_offsets = offsets[:, piece * PIECE // PER_COLUMN : (piece + 1) * PIECE // PER_COLUMN]
+            for block, stationary in enumerate((weights, identity)):
+                product = banks.tile([D, PIECE], F32, name="product")
+                nc.tensor.matmul(
+                    product[:], stationary[:], window[:].indirect(piece_offsets), start=True, stop=True
+                )
+                staged = staging.tile([D, PIECE], F32, name="staged")
+                if block == 0:
+                    nc.vector.tensor_copy(staged[:], product[:])
+                else:
+                    nc.scalar.activation(staged[:], product[:], COPY)
+                nc.sync.dma_start(out[block * D : (block + 1) * D, columns], staged[:])

@@ -9,6 +9,7 @@ V = 2048
 N = 1024
 PIECE = 512
 PER_COLUMN = 16
+WARM_UPS = 8
 
 FLOPS = 2 * D * D * N
 
@@ -28,6 +29,12 @@ def tile_documentgraph_kernel(tc, table, w, offs, out):
         nc.sync.dma_start(weights[:], w)
         identity = held.tile([D, D], BF16, name="identity")
         make_identity(nc, identity[:])
+
+        zeros = held.tile([D, PIECE], BF16, name="zeros")
+        nc.vector.memset(zeros[:], 0.0)
+        unread = banks.tile([D, PIECE], F32, name="unread")
+        for warm_up in range(WARM_UPS):
+            nc.tensor.matmul(unread[:], zeros[:, 0:D], zeros[:], start=True, stop=True)
 
         for piece in range(N // PIECE):
             columns = slice(piece * PIECE, (piece + 1) * PIECE)

@@ -7,9 +7,8 @@ COPY = mybir.ActivationFunctionType.Copy
 D = 128
 V = 2048
 N = 1024
-PIECE = 512
+PIECE = 256
 PER_COLUMN = 16
-WARM_UPS = 8
 
 FLOPS = 2 * D * D * N
 
@@ -18,8 +17,8 @@ def tile_documentgraph_kernel(tc, table, w, offs, out):
     nc = tc.nc
     with (
         tc.tile_pool(name="held", bufs=1) as held,
-        tc.tile_pool(name="staging", bufs=4) as staging,
-        tc.psum_pool(name="banks", bufs=4) as banks,
+        tc.tile_pool(name="staging", bufs=8) as staging,
+        tc.psum_pool(name="banks", bufs=8) as banks,
     ):
         offsets = held.tile([D, N // PER_COLUMN], U16, name="offsets")
         nc.sync.dma_start(offsets[:], offs)
@@ -29,12 +28,6 @@ def tile_documentgraph_kernel(tc, table, w, offs, out):
         nc.sync.dma_start(weights[:], w)
         identity = held.tile([D, D], BF16, name="identity")
         make_identity(nc, identity[:])
-
-        zeros = held.tile([D, PIECE], BF16, name="zeros")
-        nc.vector.memset(zeros[:], 0.0)
-        unread = banks.tile([D, PIECE], F32, name="unread")
-        for warm_up in range(WARM_UPS):
-            nc.tensor.matmul(unread[:], zeros[:, 0:D], zeros[:], start=True, stop=True)
 
         for piece in range(N // PIECE):
             columns = slice(piece * PIECE, (piece + 1) * PIECE)

@@ -40,6 +40,7 @@ def tile_documentgraph_kernel(tc, table, w, offs, out):
                 staged = staging.tile([D, PIECE], F32, name="staged")
                 if block == 0:
                     nc.vector.tensor_copy(staged[:], product[:])
+                    nc.sync.dma_start(out[0:D, columns], staged[:])
                 else:
                     nc.scalar.activation(staged[:], product[:], COPY)
-                nc.sync.dma_start(out[block * D : (block + 1) * D, columns], staged[:])
+                    nc.scalar.dma_start(out[D : 2 * D, columns], staged[:])

@@ -7,7 +7,8 @@ COPY = mybir.ActivationFunctionType.Copy
 D = 128
 V = 2048
 N = 1024
-PIECE = 256
+PIECES = (128, 128, 256, 256, 128, 128)
+assert sum(PIECES) == N
 PER_COLUMN = 16
 
 FLOPS = 2 * D * D * N
@@ -17,7 +18,7 @@ def tile_documentgraph_kernel(tc, table, w, offs, out):
     nc = tc.nc
     with (
         tc.tile_pool(name="held", bufs=1) as held,
-        tc.tile_pool(name="staging", bufs=8) as staging,
+        tc.tile_pool(name="staging", bufs=2 * len(PIECES)) as staging,
         tc.psum_pool(name="banks", bufs=8) as banks,
     ):
         offsets = held.tile([D, N // PER_COLUMN], U16, name="offsets")
@@ -29,18 +30,19 @@ def tile_documentgraph_kernel(tc, table, w, offs, out):
         identity = held.tile([D, D], BF16, name="identity")
         make_identity(nc, identity[:])
 
-        for piece in range(N // PIECE):
-            columns = slice(piece * PIECE, (piece + 1) * PIECE)
-            piece_offsets = offsets[:, piece * PIECE // PER_COLUMN : (piece + 1) * PIECE // PER_COLUMN]
+        first = 0
+        for entries in PIECES:
+            columns = slice(first, first + entries)
+            piece_offsets = offsets[:, first // PER_COLUMN : (first + entries) // PER_COLUMN]
+            first += entries
             for block, stationary in enumerate((weights, identity)):
-                product = banks.tile([D, PIECE], F32, name="product")
+                product = banks.tile([D, entries], F32, name="product")
                 nc.tensor.matmul(
                     product[:], stationary[:], window[:].indirect(piece_offsets), start=True, stop=True
                 )
-                staged = staging.tile([D, PIECE], F32, name="staged")
+                staged = staging.tile([D, entries], F32, name="staged")
                 if block == 0:
                     nc.vector.tensor_copy(staged[:], product[:])
-                    nc.sync.dma_start(out[0:D, columns], staged[:])
                 else:
                     nc.scalar.activation(staged[:], product[:], COPY)
-                    nc.scalar.dma_start(out[D : 2 * D, columns], staged[:])
+                nc.sync.dma_start(out[block * D : (block + 1) * D, columns], staged[:])

@@ -35,7 +35,7 @@ def tile_documentgraph_kernel(tc, table, w, offs, out):
             columns = slice(first, first + entries)
             piece_offsets = offsets[:, first // PER_COLUMN : (first + entries) // PER_COLUMN]
             first += entries
-            for block, stationary in enumerate((weights, identity)):
+            for block, stationary in ((1, identity), (0, weights)):
                 product = banks.tile([D, entries], F32, name="product")
                 nc.tensor.matmul(
                     product[:], stationary[:], window[:].indirect(piece_offsets), start=True, stop=True

@@ -2,7 +2,6 @@ import concourse.mybir as mybir
 from concourse.masks import make_identity
 
 BF16, F32, U16 = mybir.dt.bfloat16, mybir.dt.float32, mybir.dt.uint16
-COPY = mybir.ActivationFunctionType.Copy
 
 D = 128
 V = 2048
@@ -44,5 +43,5 @@ def tile_documentgraph_kernel(tc, table, w, offs, out):
                 if block == 0:
                     nc.vector.tensor_copy(staged[:], product[:])
                 else:
-                    nc.scalar.activation(staged[:], product[:], COPY)
+                    nc.scalar.copy(staged[:], product[:])
                 nc.sync.dma_start(out[block * D : (block + 1) * D, columns], staged[:])

import concourse.mybir as mybir
from concourse.masks import make_identity

BF16, F32, U16 = mybir.dt.bfloat16, mybir.dt.float32, mybir.dt.uint16

D = 128
V = 2048
N = 1024
PIECES = (128, 128, 256, 256, 128, 128)
assert sum(PIECES) == N
PER_COLUMN = 16

FLOPS = 2 * D * D * N


def tile_documentgraph_kernel(tc, table, w, offs, out):
    nc = tc.nc
    with (
        tc.tile_pool(name="held", bufs=1) as held,
        tc.tile_pool(name="staging", bufs=2 * len(PIECES)) as staging,
        tc.psum_pool(name="banks", bufs=8) as banks,
    ):
        offsets = held.tile([D, N // PER_COLUMN], U16, name="offsets")
        nc.sync.dma_start(offsets[:], offs)
        window = held.tile([D, V], BF16, name="window")
        nc.scalar.dma_start(window[:], table)
        weights = held.tile([D, D], BF16, name="weights")
        nc.sync.dma_start(weights[:], w)
        identity = held.tile([D, D], BF16, name="identity")
        make_identity(nc, identity[:])

        first = 0
        for entries in PIECES:
            columns = slice(first, first + entries)
            piece_offsets = offsets[:, first // PER_COLUMN : (first + entries) // PER_COLUMN]
            first += entries
            for block, stationary in ((1, identity), (0, weights)):
                product = banks.tile([D, entries], F32, name="product")
                nc.tensor.matmul(
                    product[:], stationary[:], window[:].indirect(piece_offsets), start=True, stop=True
                )
                staged = staging.tile([D, entries], F32, name="staged")
                if block == 0:
                    nc.vector.tensor_copy(staged[:], product[:])
                else:
                    nc.scalar.copy(staged[:], product[:])
                nc.sync.dma_start(out[block * D : (block + 1) * D, columns], staged[:])
